import numpy as np
import ml_dtypes


def mxq(x, axis, fmt="e4m3"):
    dtype, down = {"e4m3": (ml_dtypes.float8_e4m3fn, 7), "e5m2": (ml_dtypes.float8_e5m2, 14)}[fmt]
    v = np.moveaxis(np.asarray(x, np.float32).astype(ml_dtypes.bfloat16).astype(np.float64), axis, -1)
    blocks = v.reshape(v.shape[:-1] + (-1, 32))
    amax = np.abs(blocks).max(-1, keepdims=True)
    byte = np.maximum(np.where(amax > 0, np.frexp(amax)[1] - 1 + 127, 0) - down, 1)
    scale = np.exp2(byte - 127.0)
    codes = (blocks / scale).astype(np.float32).astype(dtype).astype(np.float64)
    return np.moveaxis((codes * scale).reshape(v.shape), -1, axis)


WIDE = False


def mx_kscale(k):
    if not WIDE:
        return np.ones(k)
    levels = np.array([10, -10, 5, -5, 0])
    a = np.random.permutation(np.resize(levels, k // 512 * 4)).reshape(k // 512, 4)
    idx = np.arange(k)
    return np.exp2(a[idx // 512, idx % 128 // 32])


BF16 = ml_dtypes.bfloat16


def bf(x):
    return np.asarray(x, np.float32).astype(BF16)


def f64(x):
    return np.asarray(x).astype(np.float64)


N, S, I, L, M = 128, 8, 512, 512, 256
D = I + L


def sigmoid(v):
    return 1.0 / (1.0 + np.exp(-v))


def setup_inputs():
    s = mx_kscale(D)
    r = np.random.standard_normal
    return {"modulation": bf((r((N, S, I)) * s[:I]).reshape(N, S * I)),
            "h0": bf((r((N, S, L)) * s[I:]).reshape(N, S * L)),
            "c_new": bf(0.75 * r((N, S * L))),
            "Wo": bf(r((S, L, D)) / np.sqrt(D) / s), "b_o": bf(0.3 * r((S, L))),
            "Wy": bf(r((S, M, L)) * 2.0 / np.sqrt(L)), "b_y": bf(0.2 * r((S, M)))}


def proj(aq, W, b):
    return (aq.transpose(1, 0, 2) @ mxq(f64(W), 2, "e4m3").transpose(0, 2, 1)).transpose(1, 0, 2) + f64(b)


def reference(modulation, h0, c_new, Wo, b_o, Wy, b_y):
    x = f64(modulation).reshape(N, S, I)
    h = f64(h0).reshape(N, S, L)
    c = f64(c_new).reshape(N, S, L)
    xq = mxq(np.concatenate([x, h], axis=-1), 2, "e4m3")
    o = sigmoid(proj(xq, Wo, b_o))
    h_new = o * np.tanh(c)
    y = proj(mxq(h_new, 2, "e4m3"), Wy, b_y)
    return y.reshape(N, S * M)

@@ -1,0 +1,297 @@
+from contextlib import ExitStack
+
+import concourse.mybir as mybir
+from concourse.masks import make_identity
+
+F32 = mybir.dt.float32
+BF16 = mybir.dt.bfloat16
+U32 = mybir.dt.uint32
+U8 = mybir.dt.uint8
+I32 = mybir.dt.int32
+FP8X4 = mybir.dt.float8_e4m3fn_x4
+ACTF = mybir.ActivationFunctionType
+ALU = mybir.AluOpType
+
+P = 128
+S = 8
+FLOPS = 2 * 128 * 8 * (1024 * 512 + 512 * 256)
+
+
+def tile_flatlstm_pb_kernel(tc, modulation, h0, c_new, Wo, b_o, Wy, b_y, out):
+    nc = tc.nc
+    with ExitStack() as ctx:
+        ctx.enter_context(tc.manual_schedule())
+        keep = ctx.enter_context(tc.tile_pool(name="keep", bufs=1))
+        work2 = ctx.enter_context(tc.tile_pool(name="work2", bufs=2))
+        work3 = ctx.enter_context(tc.tile_pool(name="work3", bufs=3))
+        ps_t = ctx.enter_context(tc.psum_pool(name="ps_t", bufs=5))
+        ps_o = ctx.enter_context(tc.psum_pool(name="ps_o", bufs=2))
+        ps_y = ctx.enter_context(tc.psum_pool(name="ps_y", bufs=1))
+
+        ident = keep.tile([P, P], F32)
+        ones = keep.tile([P, P], BF16)
+        by_row = keep.tile([P, 2048], BF16)
+        by_bc = keep.tile([P, 2048], BF16)
+        bo_raw = keep.tile([P, 256], BF16)
+        bo = keep.tile([P, 32], F32)
+        warm = keep.tile([P, 1], F32)
+        warm2 = keep.tile([P, 1], F32)
+        c_sb = keep.tile([P, 4096], BF16)
+        x_sb = keep.tile([P, 4096], BF16)
+        h_sb = keep.tile([P, 4096], BF16)
+        th = keep.tile([P, 4096], F32)
+        xg = keep.tile([P, 4096], BF16, align_bytes=64)
+        hg0 = keep.tile([P, 4096], BF16, align_bytes=64)
+        xc = keep.tile([P, 2048], U32, align_bytes=64)
+        xs = keep.tile([P, 2048], U8, align_bytes=64)
+        wy_sb = keep.tile([P, 8192], BF16)
+        y_sb = keep.tile([P, 2048], F32)
+        wo_sb = []
+        for s in range(S):
+            wo_t = keep.tile([P, 4096], BF16, name="wo%d" % s)
+            wo_sb.append(wo_t)
+
+        nc.vector.memset(warm[:], 0.0)
+        nc.scalar.activation(out=warm2[:], in_=warm[:], func=ACTF.Sigmoid)
+        make_identity(nc, ident[:])
+        nc.vector.memset(bo_raw[:].bitcast(I32), 0)
+        nc.vector.memset(by_row[:].bitcast(I32), 0)
+        nc.vector.memset(ones[:], 1.0)
+
+        def load_chunk(dst, src, b):
+            nc.sync.dma_start(out=dst[:, 1024 * b:1024 * (b + 1)], in_=src[:, 1024 * b:1024 * (b + 1)])
+
+        load_chunk(x_sb, modulation, 0)
+        load_chunk(c_sb, c_new, 0)
+        nc.sync.dma_start(out=bo_raw[0:16, :], in_=b_o.rearrange("s (u c) -> (s u) c", u=2))
+        nc.sync.dma_start(out=by_row[0:1, :], in_=b_y.rearrange("(o s) m -> o (s m)", o=1))
+        load_chunk(x_sb, modulation, 1)
+        load_chunk(c_sb, c_new, 1)
+        load_chunk(x_sb, modulation, 2)
+        load_chunk(x_sb, modulation, 3)
+        load_chunk(c_sb, c_new, 2)
+        load_chunk(h_sb, h0, 0)
+        load_chunk(h_sb, h0, 1)
+        load_chunk(c_sb, c_new, 3)
+        load_chunk(h_sb, h0, 2)
+        load_chunk(h_sb, h0, 3)
+        for s in range(S):
+            for k in range(2):
+                nc.sync.dma_start(
+                    out=wo_sb[s][:, 2048 * k:2048 * (k + 1)],
+                    in_=Wo[s, 256 * k:256 * (k + 1), :].rearrange("(p e) d -> p (e d)", e=2),
+                )
+            nc.sync.dma_start(
+                out=wy_sb[:, 1024 * s:1024 * (s + 1)],
+                in_=Wy[s].rearrange("(p i) l -> p (i l)", i=2),
+            )
+
+        def transpose4(words, starts):
+            bank = ps_t.tile([P, 512], F32, tag="tp", name="bank")
+            for j in range(4):
+                nc.tensor.transpose(bank[:, 128 * j:128 * (j + 1)], words[:, starts[j]:starts[j] + 128], ident[:])
+            return bank
+
+        def chunk_starts(b):
+            return [512 * b + 128 * j for j in range(4)]
+
+        def pair_copy(engine_copy, dst_bf16, col0, bank):
+            engine_copy(
+                out=dst_bf16[:].bitcast(F32)[:, col0:col0 + 512].rearrange("p (a c u) -> p a c u", a=2, u=2),
+                in_=bank[:].rearrange("p (a u c) -> p a c u", a=2, u=2),
+            )
+
+        def vcopy(out, in_):
+            nc.vector.tensor_copy(out=out, in_=in_)
+
+        def scopy(out, in_):
+            nc.scalar.copy(out=out, in_=in_)
+
+        c_w = c_sb[:].bitcast(F32)
+        x_w = x_sb[:].bitcast(F32)
+        h_w = h_sb[:].bitcast(F32)
+
+        def do_tanh(b):
+            bank = transpose4(c_w, chunk_starts(b))
+            nc.scalar.activation(
+                out=th[:, 1024 * b:1024 * (b + 1)].rearrange("p (a e n) -> p a e n", a=4, e=2),
+                in_=bank[:].bitcast(BF16).rearrange("p (a n e) -> p a e n", a=4, e=2),
+                func=ACTF.Tanh,
+            )
+
+        def do_xcopy(words, dst, b, engine_copy):
+            bank = transpose4(words, chunk_starts(b))
+            pair_copy(engine_copy, dst, 512 * b, bank)
+
+        def do_xquant(src, g, b):
+            nc.vector.quantize_mx(
+                out=xc[:, 1024 * g + 256 * b:1024 * g + 256 * (b + 1)].bitcast(FP8X4),
+                scales=xs[:, 1024 * g + 256 * b:1024 * g + 256 * (b + 1)],
+                in_=src[:, 1024 * b:1024 * (b + 1)],
+            )
+
+        def do_bo():
+            bank = ps_t.tile([P, 512], F32, tag="tp", name="bank")
+            nc.tensor.transpose(bank[:, 0:128], bo_raw[:].bitcast(F32), ident[:])
+            nc.vector.tensor_copy(out=bo[:], in_=bank[:, 0:16].bitcast(BF16))
+
+        def do_by(hf):
+            bank = ps_t.tile([P, 1024], BF16, tag="tp", name="bank")
+            for j in range(2):
+                nc.tensor.matmul(
+                    out=bank[:, 512 * j:512 * (j + 1)],
+                    lhsT=ones[:],
+                    rhs=by_row[:, 1024 * hf + 512 * j:1024 * hf + 512 * (j + 1)],
+                    start=True,
+                    stop=True,
+                )
+            nc.scalar.copy(out=by_bc[:, 1024 * hf:1024 * (hf + 1)], in_=bank[:])
+
+        do_xcopy(x_w, xg, 0, vcopy)
+        do_tanh(0)
+        do_bo()
+        do_xcopy(x_w, xg, 1, vcopy)
+        do_xquant(xg, 0, 0)
+        do_tanh(1)
+        do_by(0)
+        do_xcopy(x_w, xg, 2, vcopy)
+        do_xquant(xg, 0, 1)
+        do_xcopy(x_w, xg, 3, vcopy)
+        do_xquant(xg, 0, 2)
+        do_tanh(2)
+        do_by(1)
+        do_xcopy(h_w, hg0, 0, vcopy)
+        do_xquant(xg, 0, 3)
+        do_xcopy(h_w, hg0, 1, vcopy)
+        do_xquant(hg0, 1, 0)
+        do_tanh(3)
+        do_xcopy(h_w, hg0, 2, vcopy)
+        do_xquant(hg0, 1, 1)
+        do_xcopy(h_w, hg0, 3, scopy)
+        do_xquant(hg0, 1, 2)
+        do_xquant(hg0, 1, 3)
+
+        wg = {}
+        wc = {}
+        ws = {}
+        wyg = {}
+        wyc = {}
+        wys = {}
+        sig = {}
+        hq = {}
+        hc = {}
+        hs = {}
+        o_ps = {}
+        y_ps = {}
+
+        def wo_half(j, k):
+            words = wo_sb[j][:].bitcast(F32)
+            for g in range(2):
+                starts = [(2 * k + e) * 512 + 256 * g + 128 * u for e in range(2) for u in range(2)]
+                bank = transpose4(words, starts)
+                pair_copy(scopy, wg[j], (2 * k + g) * 512, bank)
+
+        def wo_quant(j, k):
+            nc.vector.quantize_mx(
+                out=wc[j][:, 512 * k:512 * (k + 1)].bitcast(FP8X4),
+                scales=ws[j][:, 512 * k:512 * (k + 1)],
+                in_=wg[j][:, 2048 * k:2048 * (k + 1)],
+            )
+
+        def wy_transpose_copy(j):
+            words = wy_sb[:].bitcast(F32)
+            bank = transpose4(words, [512 * j + 128 * a for a in range(4)])
+            nc.vector.tensor_copy(
+                out=wyg[j][:].bitcast(F32).rearrange("p (c a) -> p c a", a=4),
+                in_=bank[:].rearrange("p (a c) -> p c a", a=4),
+            )
+
+        def wy_quant(j):
+            nc.vector.quantize_mx(out=wyc[j][:].bitcast(FP8X4), scales=wys[j][:], in_=wyg[j][:])
+
+        def stage1(j):
+            for lt in range(4):
+                for g in range(2):
+                    col = ((2 * (lt // 2) + g) * 2 + lt % 2) * 128
+                    xcol = 1024 * g + 128 * j
+                    nc.tensor.matmul_mx(
+                        out=o_ps[j][:, 128 * lt:128 * (lt + 1)],
+                        lhsT=wc[j][:, col:col + 128].bitcast(FP8X4),
+                        lhsT_scale=ws[j][:, col:col + 128],
+                        rhs=xc[:, xcol:xcol + 128].bitcast(FP8X4),
+                        rhs_scale=xs[:, xcol:xcol + 128],
+                        start=(g == 0),
+                        stop=(g == 1),
+                    )
+
+        def sigmoid(j):
+            for lt in range(4):
+                nc.scalar.activation(
+                    out=sig[j][:, 128 * lt:128 * (lt + 1)],
+                    in_=o_ps[j][:, 128 * lt:128 * (lt + 1)],
+                    func=ACTF.Sigmoid,
+                    bias=bo[:, 4 * j + lt:4 * j + lt + 1],
+                )
+
+        def gate(j):
+            nc.vector.tensor_tensor(
+                out=hq[j][:].rearrange("p (c i t) -> p c t i", i=4, t=4),
+                in0=sig[j][:].rearrange("p (t c i) -> p c t i", t=4, i=4),
+                in1=th[:, 512 * j:512 * (j + 1)].rearrange("p (t c i) -> p c t i", t=4, i=4),
+                op=ALU.mult,
+            )
+
+        def h_quant(j):
+            nc.vector.quantize_mx(out=hc[j][:].bitcast(FP8X4), scales=hs[j][:], in_=hq[j][:])
+
+        def stage2(j):
+            nc.tensor.matmul_mx(
+                out=y_ps[j][:],
+                lhsT=hc[j][:].bitcast(FP8X4),
+                lhsT_scale=hs[j][:],
+                rhs=wyc[j][:].bitcast(FP8X4),
+                rhs_scale=wys[j][:],
+                start=True,
+                stop=True,
+            )
+
+        def finish(j):
+            cols = slice(256 * j, 256 * (j + 1))
+            nc.vector.tensor_tensor(out=y_sb[:, cols], in0=y_ps[j][:], in1=by_bc[:, cols], op=ALU.add)
+            nc.sync.dma_start(out=out[:, cols], in_=y_sb[:, cols])
+
+        for j in range(S + 2):
+            if j < S:
+                wg[j] = work2.tile([P, 4096], BF16, align_bytes=64, name="wg")
+                wc[j] = work3.tile([P, 1024], U32, align_bytes=64, name="wc")
+                ws[j] = work3.tile([P, 1024], U8, align_bytes=64, name="ws")
+                wyg[j] = work2.tile([P, 1024], BF16, align_bytes=64, name="wyg")
+                wo_half(j, 0)
+            if j >= 2:
+                hq[j - 2] = work2.tile([P, 512], BF16, align_bytes=64, name="hq")
+                hc[j - 2] = work2.tile([P, 128], U32, align_bytes=64, name="hc")
+                hs[j - 2] = work2.tile([P, 128], U8, align_bytes=64, name="hs")
+                gate(j - 2)
+            if 1 <= j <= S:
+                wyc[j - 1] = work3.tile([P, 256], U32, align_bytes=64, name="wyc")
+                wys[j - 1] = work3.tile([P, 256], U8, align_bytes=64, name="wys")
+                wy_quant(j - 1)
+            if j >= 2:
+                h_quant(j - 2)
+            if j < S:
+                wo_half(j, 1)
+                wo_quant(j, 0)
+                wy_transpose_copy(j)
+            if 1 <= j <= S:
+                o_ps[j - 1] = ps_o.tile([P, 512], F32, name="o_ps")
+                stage1(j - 1)
+            if j >= 2:
+                y_ps[j - 2] = ps_y.tile([P, 256], F32, name="y_ps")
+                stage2(j - 2)
+            if 1 <= j <= S:
+                sig[j - 1] = work2.tile([P, 512], F32, name="sig")
+                sigmoid(j - 1)
+            if j < S:
+                wo_quant(j, 1)
+            if j >= 2:
+                finish(j - 2)

@@ -25,8 +25,7 @@ def tile_flatlstm_pb_kernel(tc, modulation, h0, c_new, Wo, b_o, Wy, b_y, out):
         work2 = ctx.enter_context(tc.tile_pool(name="work2", bufs=2))
         work3 = ctx.enter_context(tc.tile_pool(name="work3", bufs=3))
         ps_t = ctx.enter_context(tc.psum_pool(name="ps_t", bufs=5))
-        ps_o = ctx.enter_context(tc.psum_pool(name="ps_o", bufs=2))
-        ps_y = ctx.enter_context(tc.psum_pool(name="ps_y", bufs=1))
+        ps_o = ctx.enter_context(tc.psum_pool(name="ps_o", bufs=3))
 
         ident = keep.tile([P, P], F32)
         ones = keep.tile([P, P], BF16)
@@ -45,12 +44,36 @@ def tile_flatlstm_pb_kernel(tc, modulation, h0, c_new, Wo, b_o, Wy, b_y, out):
         xc = keep.tile([P, 2048], U32, align_bytes=64)
         xs = keep.tile([P, 2048], U8, align_bytes=64)
         wy_sb = keep.tile([P, 8192], BF16)
+        wyc = keep.tile([P, 2048], U32, align_bytes=64)
+        wys = keep.tile([P, 2048], U8, align_bytes=64)
+        hc = keep.tile([P, 1024], U32, align_bytes=64)
+        hs = keep.tile([P, 1024], U8, align_bytes=64)
         y_sb = keep.tile([P, 2048], F32)
         wo_sb = []
         for s in range(S):
             wo_t = keep.tile([P, 4096], BF16, name="wo%d" % s)
             wo_sb.append(wo_t)
 
+        dz_in = keep.tile([P, 1024], BF16, align_bytes=64)
+        dz_c = keep.tile([P, 256], U32, align_bytes=64)
+        dz_s = keep.tile([P, 256], U8, align_bytes=64)
+        nc.vector.memset(dz_in[:].bitcast(I32), 0)
+        nc.vector.quantize_mx(out=dz_c[:].bitcast(FP8X4), scales=dz_s[:], in_=dz_in[:])
+
+        def idle_pass(bank, count):
+            for r in range(2 * count):
+                nc.tensor.matmul_mx(
+                    out=bank[:, 0:256],
+                    lhsT=dz_c[:, 0:128].bitcast(FP8X4),
+                    lhsT_scale=dz_s[:, 0:128],
+                    rhs=dz_c[:].bitcast(FP8X4),
+                    rhs_scale=dz_s[:],
+                    start=True,
+                    stop=True,
+                )
+
+        warm_bank = ps_o.tile([P, 512], F32, tag="oy", name="warm_bank")
+        idle_pass(warm_bank, 5)
         nc.vector.memset(warm[:], 0.0)
         nc.scalar.activation(out=warm2[:], in_=warm[:], func=ACTF.Sigmoid)
         make_identity(nc, ident[:])
@@ -63,10 +86,10 @@ def tile_flatlstm_pb_kernel(tc, modulation, h0, c_new, Wo, b_o, Wy, b_y, out):
 
         load_chunk(x_sb, modulation, 0)
         load_chunk(c_sb, c_new, 0)
-        nc.sync.dma_start(out=bo_raw[0:16, :], in_=b_o.rearrange("s (u c) -> (s u) c", u=2))
-        nc.sync.dma_start(out=by_row[0:1, :], in_=b_y.rearrange("(o s) m -> o (s m)", o=1))
         load_chunk(x_sb, modulation, 1)
         load_chunk(c_sb, c_new, 1)
+        nc.sync.dma_start(out=by_row[0:1, :], in_=b_y.rearrange("(o s) m -> o (s m)", o=1))
+        nc.sync.dma_start(out=bo_raw[0:16, :], in_=b_o.rearrange("s (u c) -> (s u) c", u=2))
         load_chunk(x_sb, modulation, 2)
         load_chunk(x_sb, modulation, 3)
         load_chunk(c_sb, c_new, 2)
@@ -81,6 +104,7 @@ def tile_flatlstm_pb_kernel(tc, modulation, h0, c_new, Wo, b_o, Wy, b_y, out):
                     out=wo_sb[s][:, 2048 * k:2048 * (k + 1)],
                     in_=Wo[s, 256 * k:256 * (k + 1), :].rearrange("(p e) d -> p (e d)", e=2),
                 )
+        for s in range(S):
             nc.sync.dma_start(
                 out=wy_sb[:, 1024 * s:1024 * (s + 1)],
                 in_=Wy[s].rearrange("(p i) l -> p (i l)", i=2),
@@ -135,61 +159,73 @@ def tile_flatlstm_pb_kernel(tc, modulation, h0, c_new, Wo, b_o, Wy, b_y, out):
             nc.tensor.transpose(bank[:, 0:128], bo_raw[:].bitcast(F32), ident[:])
             nc.vector.tensor_copy(out=bo[:], in_=bank[:, 0:16].bitcast(BF16))
 
-        def do_by(hf):
-            bank = ps_t.tile([P, 1024], BF16, tag="tp", name="bank")
-            for j in range(2):
-                nc.tensor.matmul(
-                    out=bank[:, 512 * j:512 * (j + 1)],
-                    lhsT=ones[:],
-                    rhs=by_row[:, 1024 * hf + 512 * j:1024 * hf + 512 * (j + 1)],
-                    start=True,
-                    stop=True,
-                )
-            nc.scalar.copy(out=by_bc[:, 1024 * hf:1024 * (hf + 1)], in_=bank[:])
+        by_bank = {}
+
+        def do_by(q):
+            if q % 4 == 0:
+                by_bank[q // 4] = ps_o.tile([P, 1024], BF16, tag="oy", name="by_bank")
+            bank = by_bank[q // 4]
+            src = q % 8
+            nc.tensor.matmul(
+                out=bank[:, 256 * (q % 4):256 * (q % 4 + 1)],
+                lhsT=ones[:],
+                rhs=by_row[:, 256 * src:256 * (src + 1)],
+                start=True,
+                stop=True,
+            )
+            if q in (3, 7):
+                nc.scalar.copy(out=by_bc[:, 1024 * (q // 4):1024 * (q // 4 + 1)], in_=bank[:])
 
         do_xcopy(x_w, xg, 0, vcopy)
         do_tanh(0)
-        do_bo()
         do_xcopy(x_w, xg, 1, vcopy)
+        do_by(0)
         do_xquant(xg, 0, 0)
         do_tanh(1)
-        do_by(0)
+        do_by(1)
+        do_bo()
         do_xcopy(x_w, xg, 2, vcopy)
+        do_by(2)
         do_xquant(xg, 0, 1)
         do_xcopy(x_w, xg, 3, vcopy)
+        do_by(3)
         do_xquant(xg, 0, 2)
         do_tanh(2)
-        do_by(1)
+        do_by(4)
         do_xcopy(h_w, hg0, 0, vcopy)
+        do_by(5)
         do_xquant(xg, 0, 3)
         do_xcopy(h_w, hg0, 1, vcopy)
+        do_by(6)
         do_xquant(hg0, 1, 0)
         do_tanh(3)
+        do_by(7)
         do_xcopy(h_w, hg0, 2, vcopy)
+        do_by(8)
         do_xquant(hg0, 1, 1)
         do_xcopy(h_w, hg0, 3, scopy)
+        do_by(9)
         do_xquant(hg0, 1, 2)
         do_xquant(hg0, 1, 3)
+        post_bank = ps_o.tile([P, 512], F32, tag="oy", name="post_bank")
+        idle_pass(post_bank, 2)
 
+        EXTRA = [1,1,1,1,1,1,1,1]
+        YEXTRA = [1,0,1,0,0,0,0,0]
         wg = {}
         wc = {}
         ws = {}
         wyg = {}
-        wyc = {}
-        wys = {}
         sig = {}
         hq = {}
-        hc = {}
-        hs = {}
         o_ps = {}
         y_ps = {}
 
-        def wo_half(j, k):
+        def wo_bank(j, k, g, engine_copy):
             words = wo_sb[j][:].bitcast(F32)
-            for g in range(2):
-                starts = [(2 * k + e) * 512 + 256 * g + 128 * u for e in range(2) for u in range(2)]
-                bank = transpose4(words, starts)
-                pair_copy(scopy, wg[j], (2 * k + g) * 512, bank)
+            starts = [(2 * k + e) * 512 + 256 * g + 128 * u for e in range(2) for u in range(2)]
+            bank = transpose4(words, starts)
+            pair_copy(engine_copy, wg[j], (2 * k + g) * 512, bank)
 
         def wo_quant(j, k):
             nc.vector.quantize_mx(
@@ -198,18 +234,22 @@ def tile_flatlstm_pb_kernel(tc, modulation, h0, c_new, Wo, b_o, Wy, b_y, out):
                 in_=wg[j][:, 2048 * k:2048 * (k + 1)],
             )
 
-        def wy_transpose_copy(j):
+        def wy_transpose_copy(j, engine_copy):
+            wyg[j] = work3.tile([P, 1024], BF16, align_bytes=64, name="wyg")
             words = wy_sb[:].bitcast(F32)
             bank = transpose4(words, [512 * j + 128 * a for a in range(4)])
-            nc.vector.tensor_copy(
+            engine_copy(
                 out=wyg[j][:].bitcast(F32).rearrange("p (c a) -> p c a", a=4),
                 in_=bank[:].rearrange("p (a c) -> p c a", a=4),
             )
 
         def wy_quant(j):
-            nc.vector.quantize_mx(out=wyc[j][:].bitcast(FP8X4), scales=wys[j][:], in_=wyg[j][:])
+            cols = slice(256 * j, 256 * (j + 1))
+            nc.vector.quantize_mx(out=wyc[:, cols].bitcast(FP8X4), scales=wys[:, cols], in_=wyg[j][:])
 
         def stage1(j):
+            o_ps[j] = ps_o.tile([P, 512], F32, tag="oy", name="o_ps")
+            idle_pass(o_ps[j], EXTRA[j])
             for lt in range(4):
                 for g in range(2):
                     col = ((2 * (lt // 2) + g) * 2 + lt % 2) * 128
@@ -225,6 +265,7 @@ def tile_flatlstm_pb_kernel(tc, modulation, h0, c_new, Wo, b_o, Wy, b_y, out):
                     )
 
         def sigmoid(j):
+            sig[j] = work2.tile([P, 512], F32, name="sig")
             for lt in range(4):
                 nc.scalar.activation(
                     out=sig[j][:, 128 * lt:128 * (lt + 1)],
@@ -234,6 +275,7 @@ def tile_flatlstm_pb_kernel(tc, modulation, h0, c_new, Wo, b_o, Wy, b_y, out):
                 )
 
         def gate(j):
+            hq[j] = work2.tile([P, 512], BF16, align_bytes=64, name="hq")
             nc.vector.tensor_tensor(
                 out=hq[j][:].rearrange("p (c i t) -> p c t i", i=4, t=4),
                 in0=sig[j][:].rearrange("p (t c i) -> p c t i", t=4, i=4),
@@ -242,56 +284,90 @@ def tile_flatlstm_pb_kernel(tc, modulation, h0, c_new, Wo, b_o, Wy, b_y, out):
             )
 
         def h_quant(j):
-            nc.vector.quantize_mx(out=hc[j][:].bitcast(FP8X4), scales=hs[j][:], in_=hq[j][:])
+            cols = slice(128 * j, 128 * (j + 1))
+            nc.vector.quantize_mx(out=hc[:, cols].bitcast(FP8X4), scales=hs[:, cols], in_=hq[j][:])
 
         def stage2(j):
+            y_ps[j] = ps_o.tile([P, 512], F32, tag="oy", name="y_ps")
+            idle_pass(y_ps[j], YEXTRA[j])
             nc.tensor.matmul_mx(
-                out=y_ps[j][:],
-                lhsT=hc[j][:].bitcast(FP8X4),
-                lhsT_scale=hs[j][:],
-                rhs=wyc[j][:].bitcast(FP8X4),
-                rhs_scale=wys[j][:],
+                out=y_ps[j][:, 0:256],
+                lhsT=hc[:, 128 * j:128 * (j + 1)].bitcast(FP8X4),
+                lhsT_scale=hs[:, 128 * j:128 * (j + 1)],
+                rhs=wyc[:, 256 * j:256 * (j + 1)].bitcast(FP8X4),
+                rhs_scale=wys[:, 256 * j:256 * (j + 1)],
                 start=True,
                 stop=True,
             )
 
         def finish(j):
             cols = slice(256 * j, 256 * (j + 1))
-            nc.vector.tensor_tensor(out=y_sb[:, cols], in0=y_ps[j][:], in1=by_bc[:, cols], op=ALU.add)
+            nc.vector.tensor_tensor(out=y_sb[:, cols], in0=y_ps[j][:, 0:256], in1=by_bc[:, cols], op=ALU.add)
             nc.sync.dma_start(out=out[:, cols], in_=y_sb[:, cols])
 
-        for j in range(S + 2):
-            if j < S:
-                wg[j] = work2.tile([P, 4096], BF16, align_bytes=64, name="wg")
-                wc[j] = work3.tile([P, 1024], U32, align_bytes=64, name="wc")
-                ws[j] = work3.tile([P, 1024], U8, align_bytes=64, name="ws")
-                wyg[j] = work2.tile([P, 1024], BF16, align_bytes=64, name="wyg")
-                wo_half(j, 0)
-            if j >= 2:
-                hq[j - 2] = work2.tile([P, 512], BF16, align_bytes=64, name="hq")
-                hc[j - 2] = work2.tile([P, 128], U32, align_bytes=64, name="hc")
-                hs[j - 2] = work2.tile([P, 128], U8, align_bytes=64, name="hs")
-                gate(j - 2)
-            if 1 <= j <= S:
-                wyc[j - 1] = work3.tile([P, 256], U32, align_bytes=64, name="wyc")
-                wys[j - 1] = work3.tile([P, 256], U8, align_bytes=64, name="wys")
-                wy_quant(j - 1)
-            if j >= 2:
-                h_quant(j - 2)
-            if j < S:
-                wo_half(j, 1)
-                wo_quant(j, 0)
-                wy_transpose_copy(j)
-            if 1 <= j <= S:
-                o_ps[j - 1] = ps_o.tile([P, 512], F32, name="o_ps")
-                stage1(j - 1)
-            if j >= 2:
-                y_ps[j - 2] = ps_y.tile([P, 256], F32, name="y_ps")
-                stage2(j - 2)
-            if 1 <= j <= S:
-                sig[j - 1] = work2.tile([P, 512], F32, name="sig")
-                sigmoid(j - 1)
-            if j < S:
-                wo_quant(j, 1)
-            if j >= 2:
-                finish(j - 2)
+        MID = [2,1,0,0,0,0,0,0]
+        DVE_BANKS = [[2],[2],[2],[2],[2],[2],[2],[2]]
+
+        def wo_round(i):
+            wg[i] = work2.tile([P, 4096], BF16, align_bytes=64, name="wg")
+            wc[i] = work3.tile([P, 1024], U32, align_bytes=64, name="wc")
+            ws[i] = work3.tile([P, 1024], U8, align_bytes=64, name="ws")
+            for b in range(4):
+                wo_bank(i, b // 2, b % 2, vcopy if b in DVE_BANKS[i] else scopy)
+                if b == 1 and MID[i] > 0:
+                    mid_bank = ps_o.tile([P, 512], F32, tag="oy", name="mid_bank")
+                    idle_pass(mid_bank, MID[i])
+
+        for i in range(S):
+            wo_round(i)
+            if i == 0:
+                fill_bank = ps_o.tile([P, 512], F32, tag="oy", name="fill_bank")
+                idle_pass(fill_bank, 2)
+            if i >= 1:
+                stage1(i - 1)
+                sigmoid(i - 1)
+            if i >= 2:
+                gate(i - 2)
+            wo_quant(i, 0)
+            if i >= 2:
+                h_quant(i - 2)
+            wo_quant(i, 1)
+
+        wy_transpose_copy(0, scopy)
+        wy_transpose_copy(1, scopy)
+        wy_quant(0)
+        wy_transpose_copy(2, scopy)
+        wy_transpose_copy(3, scopy)
+        stage1(7)
+        stage2(0)
+        sigmoid(7)
+        wy_quant(1)
+        gate(6)
+        wy_quant(2)
+        h_quant(6)
+        finish(0)
+        wy_transpose_copy(4, scopy)
+        wy_transpose_copy(5, scopy)
+        wy_quant(3)
+        stage2(1)
+        stage2(2)
+        stage2(3)
+        gate(7)
+        finish(1)
+        h_quant(7)
+        finish(2)
+        wy_transpose_copy(6, scopy)
+        wy_transpose_copy(7, scopy)
+        wy_quant(4)
+        finish(3)
+        wy_quant(5)
+        stage2(4)
+        stage2(5)
+        wy_quant(6)
+        finish(4)
+        wy_quant(7)
+        finish(5)
+        stage2(6)
+        stage2(7)
+        finish(6)
+        finish(7)

from contextlib import ExitStack

import concourse.mybir as mybir
from concourse.masks import make_identity

F32 = mybir.dt.float32
BF16 = mybir.dt.bfloat16
U32 = mybir.dt.uint32
U8 = mybir.dt.uint8
I32 = mybir.dt.int32
FP8X4 = mybir.dt.float8_e4m3fn_x4
ACTF = mybir.ActivationFunctionType
ALU = mybir.AluOpType

P = 128
S = 8
FLOPS = 2 * 128 * 8 * (1024 * 512 + 512 * 256)


def tile_flatlstm_pb_kernel(tc, modulation, h0, c_new, Wo, b_o, Wy, b_y, out):
    nc = tc.nc
    with ExitStack() as ctx:
        ctx.enter_context(tc.manual_schedule())
        keep = ctx.enter_context(tc.tile_pool(name="keep", bufs=1))
        work2 = ctx.enter_context(tc.tile_pool(name="work2", bufs=2))
        work3 = ctx.enter_context(tc.tile_pool(name="work3", bufs=3))
        ps_t = ctx.enter_context(tc.psum_pool(name="ps_t", bufs=5))
        ps_o = ctx.enter_context(tc.psum_pool(name="ps_o", bufs=3))

        ident = keep.tile([P, P], F32)
        ones = keep.tile([P, P], BF16)
        by_row = keep.tile([P, 2048], BF16)
        by_bc = keep.tile([P, 2048], BF16)
        bo_raw = keep.tile([P, 256], BF16)
        bo = keep.tile([P, 32], F32)
        warm = keep.tile([P, 1], F32)
        warm2 = keep.tile([P, 1], F32)
        c_sb = keep.tile([P, 4096], BF16)
        x_sb = keep.tile([P, 4096], BF16)
        h_sb = keep.tile([P, 4096], BF16)
        th = keep.tile([P, 4096], F32)
        xg = keep.tile([P, 4096], BF16, align_bytes=64)
        hg0 = keep.tile([P, 4096], BF16, align_bytes=64)
        xc = keep.tile([P, 2048], U32, align_bytes=64)
        xs = keep.tile([P, 2048], U8, align_bytes=64)
        wy_sb = keep.tile([P, 8192], BF16)
        wyc = keep.tile([P, 2048], U32, align_bytes=64)
        wys = keep.tile([P, 2048], U8, align_bytes=64)
        hc = keep.tile([P, 1024], U32, align_bytes=64)
        hs = keep.tile([P, 1024], U8, align_bytes=64)
        y_sb = keep.tile([P, 2048], F32)
        wo_sb = []
        for s in range(S):
            wo_t = keep.tile([P, 4096], BF16, name="wo%d" % s)
            wo_sb.append(wo_t)

        dz_in = keep.tile([P, 1024], BF16, align_bytes=64)
        dz_c = keep.tile([P, 256], U32, align_bytes=64)
        dz_s = keep.tile([P, 256], U8, align_bytes=64)
        nc.vector.memset(dz_in[:].bitcast(I32), 0)
        nc.vector.quantize_mx(out=dz_c[:].bitcast(FP8X4), scales=dz_s[:], in_=dz_in[:])

        def idle_pass(bank, count):
            for r in range(2 * count):
                nc.tensor.matmul_mx(
                    out=bank[:, 0:256],
                    lhsT=dz_c[:, 0:128].bitcast(FP8X4),
                    lhsT_scale=dz_s[:, 0:128],
                    rhs=dz_c[:].bitcast(FP8X4),
                    rhs_scale=dz_s[:],
                    start=True,
                    stop=True,
                )

        warm_bank = ps_o.tile([P, 512], F32, tag="oy", name="warm_bank")
        idle_pass(warm_bank, 5)
        nc.vector.memset(warm[:], 0.0)
        nc.scalar.activation(out=warm2[:], in_=warm[:], func=ACTF.Sigmoid)
        make_identity(nc, ident[:])
        nc.vector.memset(bo_raw[:].bitcast(I32), 0)
        nc.vector.memset(by_row[:].bitcast(I32), 0)
        nc.vector.memset(ones[:], 1.0)

        def load_chunk(dst, src, b):
            nc.sync.dma_start(out=dst[:, 1024 * b:1024 * (b + 1)], in_=src[:, 1024 * b:1024 * (b + 1)])

        load_chunk(x_sb, modulation, 0)
        load_chunk(c_sb, c_new, 0)
        load_chunk(x_sb, modulation, 1)
        load_chunk(c_sb, c_new, 1)
        nc.sync.dma_start(out=by_row[0:1, :], in_=b_y.rearrange("(o s) m -> o (s m)", o=1))
        nc.sync.dma_start(out=bo_raw[0:16, :], in_=b_o.rearrange("s (u c) -> (s u) c", u=2))
        load_chunk(x_sb, modulation, 2)
        load_chunk(x_sb, modulation, 3)
        load_chunk(c_sb, c_new, 2)
        load_chunk(h_sb, h0, 0)
        load_chunk(h_sb, h0, 1)
        load_chunk(c_sb, c_new, 3)
        load_chunk(h_sb, h0, 2)
        load_chunk(h_sb, h0, 3)
        for s in range(S):
            for k in range(2):
                nc.sync.dma_start(
                    out=wo_sb[s][:, 2048 * k:2048 * (k + 1)],
                    in_=Wo[s, 256 * k:256 * (k + 1), :].rearrange("(p e) d -> p (e d)", e=2),
                )
        for s in range(S):
            nc.sync.dma_start(
                out=wy_sb[:, 1024 * s:1024 * (s + 1)],
                in_=Wy[s].rearrange("(p i) l -> p (i l)", i=2),
            )

        def transpose4(words, starts):
            bank = ps_t.tile([P, 512], F32, tag="tp", name="bank")
            for j in range(4):
                nc.tensor.transpose(bank[:, 128 * j:128 * (j + 1)], words[:, starts[j]:starts[j] + 128], ident[:])
            return bank

        def chunk_starts(b):
            return [512 * b + 128 * j for j in range(4)]

        def pair_copy(engine_copy, dst_bf16, col0, bank):
            engine_copy(
                out=dst_bf16[:].bitcast(F32)[:, col0:col0 + 512].rearrange("p (a c u) -> p a c u", a=2, u=2),
                in_=bank[:].rearrange("p (a u c) -> p a c u", a=2, u=2),
            )

        def vcopy(out, in_):
            nc.vector.tensor_copy(out=out, in_=in_)

        def scopy(out, in_):
            nc.scalar.copy(out=out, in_=in_)

        c_w = c_sb[:].bitcast(F32)
        x_w = x_sb[:].bitcast(F32)
        h_w = h_sb[:].bitcast(F32)

        def do_tanh(b):
            bank = transpose4(c_w, chunk_starts(b))
            nc.scalar.activation(
                out=th[:, 1024 * b:1024 * (b + 1)].rearrange("p (a e n) -> p a e n", a=4, e=2),
                in_=bank[:].bitcast(BF16).rearrange("p (a n e) -> p a e n", a=4, e=2),
                func=ACTF.Tanh,
            )

        def do_xcopy(words, dst, b, engine_copy):
            bank = transpose4(words, chunk_starts(b))
            pair_copy(engine_copy, dst, 512 * b, bank)

        def do_xquant(src, g, b):
            nc.vector.quantize_mx(
                out=xc[:, 1024 * g + 256 * b:1024 * g + 256 * (b + 1)].bitcast(FP8X4),
                scales=xs[:, 1024 * g + 256 * b:1024 * g + 256 * (b + 1)],
                in_=src[:, 1024 * b:1024 * (b + 1)],
            )

        def do_bo():
            bank = ps_t.tile([P, 512], F32, tag="tp", name="bank")
            nc.tensor.transpose(bank[:, 0:128], bo_raw[:].bitcast(F32), ident[:])
            nc.vector.tensor_copy(out=bo[:], in_=bank[:, 0:16].bitcast(BF16))

        by_bank = {}

        def do_by(q):
            if q % 4 == 0:
                by_bank[q // 4] = ps_o.tile([P, 1024], BF16, tag="oy", name="by_bank")
            bank = by_bank[q // 4]
            src = q % 8
            nc.tensor.matmul(
                out=bank[:, 256 * (q % 4):256 * (q % 4 + 1)],
                lhsT=ones[:],
                rhs=by_row[:, 256 * src:256 * (src + 1)],
                start=True,
                stop=True,
            )
            if q in (3, 7):
                nc.scalar.copy(out=by_bc[:, 1024 * (q // 4):1024 * (q // 4 + 1)], in_=bank[:])

        do_xcopy(x_w, xg, 0, vcopy)
        do_tanh(0)
        do_xcopy(x_w, xg, 1, vcopy)
        do_by(0)
        do_xquant(xg, 0, 0)
        do_tanh(1)
        do_by(1)
        do_bo()
        do_xcopy(x_w, xg, 2, vcopy)
        do_by(2)
        do_xquant(xg, 0, 1)
        do_xcopy(x_w, xg, 3, vcopy)
        do_by(3)
        do_xquant(xg, 0, 2)
        do_tanh(2)
        do_by(4)
        do_xcopy(h_w, hg0, 0, vcopy)
        do_by(5)
        do_xquant(xg, 0, 3)
        do_xcopy(h_w, hg0, 1, vcopy)
        do_by(6)
        do_xquant(hg0, 1, 0)
        do_tanh(3)
        do_by(7)
        do_xcopy(h_w, hg0, 2, vcopy)
        do_by(8)
        do_xquant(hg0, 1, 1)
        do_xcopy(h_w, hg0, 3, scopy)
        do_by(9)
        do_xquant(hg0, 1, 2)
        do_xquant(hg0, 1, 3)
        post_bank = ps_o.tile([P, 512], F32, tag="oy", name="post_bank")
        idle_pass(post_bank, 2)

        EXTRA = [1,1,1,1,1,1,1,1]
        YEXTRA = [1,0,1,0,0,0,0,0]
        wg = {}
        wc = {}
        ws = {}
        wyg = {}
        sig = {}
        hq = {}
        o_ps = {}
        y_ps = {}

        def wo_bank(j, k, g, engine_copy):
            words = wo_sb[j][:].bitcast(F32)
            starts = [(2 * k + e) * 512 + 256 * g + 128 * u for e in range(2) for u in range(2)]
            bank = transpose4(words, starts)
            pair_copy(engine_copy, wg[j], (2 * k + g) * 512, bank)

        def wo_quant(j, k):
            nc.vector.quantize_mx(
                out=wc[j][:, 512 * k:512 * (k + 1)].bitcast(FP8X4),
                scales=ws[j][:, 512 * k:512 * (k + 1)],
                in_=wg[j][:, 2048 * k:2048 * (k + 1)],
            )

        def wy_transpose_copy(j, engine_copy):
            wyg[j] = work3.tile([P, 1024], BF16, align_bytes=64, name="wyg")
            words = wy_sb[:].bitcast(F32)
            bank = transpose4(words, [512 * j + 128 * a for a in range(4)])
            engine_copy(
                out=wyg[j][:].bitcast(F32).rearrange("p (c a) -> p c a", a=4),
                in_=bank[:].rearrange("p (a c) -> p c a", a=4),
            )

        def wy_quant(j):
            cols = slice(256 * j, 256 * (j + 1))
            nc.vector.quantize_mx(out=wyc[:, cols].bitcast(FP8X4), scales=wys[:, cols], in_=wyg[j][:])

        def stage1(j):
            o_ps[j] = ps_o.tile([P, 512], F32, tag="oy", name="o_ps")
            idle_pass(o_ps[j], EXTRA[j])
            for lt in range(4):
                for g in range(2):
                    col = ((2 * (lt // 2) + g) * 2 + lt % 2) * 128
                    xcol = 1024 * g + 128 * j
                    nc.tensor.matmul_mx(
                        out=o_ps[j][:, 128 * lt:128 * (lt + 1)],
                        lhsT=wc[j][:, col:col + 128].bitcast(FP8X4),
                        lhsT_scale=ws[j][:, col:col + 128],
                        rhs=xc[:, xcol:xcol + 128].bitcast(FP8X4),
                        rhs_scale=xs[:, xcol:xcol + 128],
                        start=(g == 0),
                        stop=(g == 1),
                    )

        def sigmoid(j):
            sig[j] = work2.tile([P, 512], F32, name="sig")
            for lt in range(4):
                nc.scalar.activation(
                    out=sig[j][:, 128 * lt:128 * (lt + 1)],
                    in_=o_ps[j][:, 128 * lt:128 * (lt + 1)],
                    func=ACTF.Sigmoid,
                    bias=bo[:, 4 * j + lt:4 * j + lt + 1],
                )

        def gate(j):
            hq[j] = work2.tile([P, 512], BF16, align_bytes=64, name="hq")
            nc.vector.tensor_tensor(
                out=hq[j][:].rearrange("p (c i t) -> p c t i", i=4, t=4),
                in0=sig[j][:].rearrange("p (t c i) -> p c t i", t=4, i=4),
                in1=th[:, 512 * j:512 * (j + 1)].rearrange("p (t c i) -> p c t i", t=4, i=4),
                op=ALU.mult,
            )

        def h_quant(j):
            cols = slice(128 * j, 128 * (j + 1))
            nc.vector.quantize_mx(out=hc[:, cols].bitcast(FP8X4), scales=hs[:, cols], in_=hq[j][:])

        def stage2(j):
            y_ps[j] = ps_o.tile([P, 512], F32, tag="oy", name="y_ps")
            idle_pass(y_ps[j], YEXTRA[j])
            nc.tensor.matmul_mx(
                out=y_ps[j][:, 0:256],
                lhsT=hc[:, 128 * j:128 * (j + 1)].bitcast(FP8X4),
                lhsT_scale=hs[:, 128 * j:128 * (j + 1)],
                rhs=wyc[:, 256 * j:256 * (j + 1)].bitcast(FP8X4),
                rhs_scale=wys[:, 256 * j:256 * (j + 1)],
                start=True,
                stop=True,
            )

        def finish(j):
            cols = slice(256 * j, 256 * (j + 1))
            nc.vector.tensor_tensor(out=y_sb[:, cols], in0=y_ps[j][:, 0:256], in1=by_bc[:, cols], op=ALU.add)
            nc.sync.dma_start(out=out[:, cols], in_=y_sb[:, cols])

        MID = [2,1,0,0,0,0,0,0]
        DVE_BANKS = [[2],[2],[2],[2],[2],[2],[2],[2]]

        def wo_round(i):
            wg[i] = work2.tile([P, 4096], BF16, align_bytes=64, name="wg")
            wc[i] = work3.tile([P, 1024], U32, align_bytes=64, name="wc")
            ws[i] = work3.tile([P, 1024], U8, align_bytes=64, name="ws")
            for b in range(4):
                wo_bank(i, b // 2, b % 2, vcopy if b in DVE_BANKS[i] else scopy)
                if b == 1 and MID[i] > 0:
                    mid_bank = ps_o.tile([P, 512], F32, tag="oy", name="mid_bank")
                    idle_pass(mid_bank, MID[i])

        for i in range(S):
            wo_round(i)
            if i == 0:
                fill_bank = ps_o.tile([P, 512], F32, tag="oy", name="fill_bank")
                idle_pass(fill_bank, 2)
            if i >= 1:
                stage1(i - 1)
                sigmoid(i - 1)
            if i >= 2:
                gate(i - 2)
            wo_quant(i, 0)
            if i >= 2:
                h_quant(i - 2)
            wo_quant(i, 1)

        wy_transpose_copy(0, scopy)
        wy_transpose_copy(1, scopy)
        wy_quant(0)
        wy_transpose_copy(2, scopy)
        wy_transpose_copy(3, scopy)
        stage1(7)
        stage2(0)
        sigmoid(7)
        wy_quant(1)
        gate(6)
        wy_quant(2)
        h_quant(6)
        finish(0)
        wy_transpose_copy(4, scopy)
        wy_transpose_copy(5, scopy)
        wy_quant(3)
        stage2(1)
        stage2(2)
        stage2(3)
        gate(7)
        finish(1)
        h_quant(7)
        finish(2)
        wy_transpose_copy(6, scopy)
        wy_transpose_copy(7, scopy)
        wy_quant(4)
        finish(3)
        wy_quant(5)
        stage2(4)
        stage2(5)
        wy_quant(6)
        finish(4)
        wy_quant(7)
        finish(5)
        stage2(6)
        stage2(7)
        finish(6)
        finish(7)
